import numpy as np
import ml_dtypes


def mxq(x, axis, fmt="e4m3"):
    dtype, down = {"e4m3": (ml_dtypes.float8_e4m3fn, 7), "e5m2": (ml_dtypes.float8_e5m2, 14)}[fmt]
    v = np.moveaxis(np.asarray(x, np.float32).astype(ml_dtypes.bfloat16).astype(np.float64), axis, -1)
    blocks = v.reshape(v.shape[:-1] + (-1, 32))
    amax = np.abs(blocks).max(-1, keepdims=True)
    byte = np.maximum(np.where(amax > 0, np.frexp(amax)[1] - 1 + 127, 0) - down, 1)
    scale = np.exp2(byte - 127.0)
    codes = (blocks / scale).astype(np.float32).astype(dtype).astype(np.float64)
    return np.moveaxis((codes * scale).reshape(v.shape), -1, axis)


WIDE = False


def mx_kscale(k):
    if not WIDE:
        return np.ones(k)
    levels = np.array([30, -30])
    if k % 512:
        return np.exp2(np.random.permutation(np.resize(levels, k // 32))).repeat(32)
    a = np.empty((k // 512, 16))
    for p in range(k // 512):
        a[p, :8] = np.random.permutation(np.resize(levels, 8))
        for g in range(8):
            far = levels[np.abs(levels - a[p, g]) >= 10]
            a[p, g + 8] = far[np.random.randint(len(far))]
    return np.exp2(a.ravel()).repeat(32)


BF16 = ml_dtypes.bfloat16


def bf(x):
    return np.asarray(x, np.float32).astype(BF16)


def f64(x):
    return np.asarray(x).astype(np.float64)


B, S, E, H, KVH, HD = 1, 512, 2048, 16, 4, 128
THETA = 10000.0


def apply_rope(t, cos, sin):
    x1, x2 = np.split(t, 2, axis=-1)
    c = cos[None, None, :, :]
    s = sin[None, None, :, :]
    return np.concatenate([x1 * c - x2 * s, x2 * c + x1 * s], axis=-1)


def setup_inputs():
    s = mx_kscale(E)
    inv_freq = 1.0 / THETA ** (np.arange(0, HD, 2) / HD)
    pos = np.random.randint(0, S) + np.arange(S)
    ang = pos[:, None] * inv_freq[None, :]
    return {"x": bf(np.random.standard_normal((B, S, E)) * s),
            "Wq": bf(np.random.standard_normal((H * HD, E)) * 1.3 / np.sqrt(E) / s[None, :]),
            "bq": bf(np.random.standard_normal(H * HD) * 0.3),
            "Wkv": bf(np.random.standard_normal((2 * KVH * HD, E)) * 1.3 / np.sqrt(E) / s[None, :]),
            "bkv": bf(np.random.standard_normal(2 * KVH * HD) * 0.3),
            "cos": bf(np.cos(ang)),
            "sin": bf(np.sin(ang))}


def reference(x, Wq, bq, Wkv, bkv, cos, sin):
    xq = mxq(f64(x), 2, "e5m2")
    q = (xq @ mxq(f64(Wq), 1, "e5m2").T) + f64(bq)
    kv = (xq @ mxq(f64(Wkv), 1, "e5m2").T) + f64(bkv)
    k, v = np.split(kv, 2, axis=-1)
    q = q.reshape(B, S, H, HD).transpose(0, 2, 1, 3)
    k = k.reshape(B, S, KVH, HD).transpose(0, 2, 1, 3)
    v = v.reshape(B, S, KVH, HD).transpose(0, 2, 1, 3)
    q_rot = apply_rope(q, f64(cos), f64(sin))
    k_rot = apply_rope(k, f64(cos), f64(sin))
    return q_rot, k_rot, v

@@ -1,0 +1,270 @@
+from contextlib import ExitStack
+
+import concourse.mybir as mybir
+from concourse.masks import make_identity
+
+S, E, HD = 512, 2048, 128
+FLOPS = 2 * S * E * 3072
+
+F32 = mybir.dt.float32
+BF16 = mybir.dt.bfloat16
+U32 = mybir.dt.uint32
+U8 = mybir.dt.uint8
+E5M2X4 = mybir.dt.float8_e5m2_x4
+ADD = mybir.AluOpType.add
+SUB = mybir.AluOpType.subtract
+MULT = mybir.AluOpType.mult
+
+P = 128
+HALF = HD // 2
+BANK = 512
+PAIRS = 12
+ROPE_PAIRS = 10
+Q_PAIRS = 8
+PAIR_ROWS = 2 * HD
+UNIT_K = 1024
+TILES = 2 * PAIRS
+ROPE_TILES = 2 * ROPE_PAIRS
+
+VECTOR_SORTED = (0, 1, 2, 3, 4, 5, 6, 7)
+SCALAR_SORTED = (0, 1, 2)
+SCALAR_SORT_FROM = 10
+SORT_AHEAD = 4
+SORT_NOT_BEFORE = 9
+ROT_LAG = 1
+LAG_STEP = 99
+LOAD_AHEAD = 10
+POOL_ADD = True
+POOL_COS_EVERY = 0
+EARLY_BIAS = 2
+HEAD_LEAD = 3.0
+TABLE_KEY = -0.5
+LEAD_UNTIL = 12
+SLOT0 = 5
+SLOT1 = 7
+EARLY_ROT = 2
+RUN_FROM = 10
+T_OFF = 7
+WIDE_FROM = 99
+
+
+def tile_qwen2attention_pa_kernel(tc, x, Wq, bq, Wkv, bkv, cos, sin, out_0, out_1, out_2):
+    nc = tc.nc
+    with ExitStack() as ctx:
+        sb = ctx.enter_context(tc.tile_pool(name="sb", bufs=1))
+        ps = ctx.enter_context(tc.psum_pool(name="ps", bufs=1))
+        ctx.enter_context(tc.manual_schedule())
+
+        def ring(name, count, shape, dtype):
+            return [sb.tile(shape, dtype, name="%s%d" % (name, i), align_bytes=64) for i in range(count)]
+
+        def banks(name, count):
+            return [ps.tile([P, BANK], F32, name="%s%d" % (name, i)) for i in range(count)]
+
+        units = [("x", 0, 0), ("w", 0, 0), ("x", 0, 1), ("w", 0, 1), ("x", 1, 0), ("x", 1, 1)]
+        units = units + [("w", q, kh) for q in range(1, PAIRS) for kh in range(2)]
+        x_rows = x[0].rearrange("(p j) k -> p j k", j=4)
+
+        def w_rows(q):
+            w, q0 = (Wq, q) if q < Q_PAIRS else (Wkv, q - Q_PAIRS)
+            return w[q0 * PAIR_ROWS : (q0 + 1) * PAIR_ROWS, :].rearrange("(r p) k -> p r k", p=P)
+
+        def out_rows(q):
+            o, q0 = (out_0, q) if q < Q_PAIRS else (out_1, q - Q_PAIRS) if q < ROPE_PAIRS else (out_2, q - ROPE_PAIRS)
+            return o[0, 2 * q0 : 2 * q0 + 2].rearrange("h (p j) d -> p h j d", j=4)
+
+        ident_f32 = sb.tile([P, P], F32, name="ident_f32", align_bytes=64)
+        ident_bf16 = sb.tile([P, P], BF16, name="ident_bf16", align_bytes=64)
+        bias_rows = sb.tile([P, BANK], BF16, name="bias_rows", align_bytes=64)
+        cos_sin = sb.tile([P, 2, 4, HALF], BF16, name="cos_sin", align_bytes=64)
+        bias = ring("bias", PAIRS // 2, [P, 2, PAIR_ROWS], BF16)
+        sorted_words = ring("sorted", SORT_AHEAD, [P, 4, 2, P], F32)
+        grouped = ring("grouped", 4, [P, 4 * BANK], BF16)
+        x_codes = ring("x_codes", 4, [P, BANK], U32)
+        x_scales = ring("x_scales", 4, [P, BANK], U8)
+        w_codes = ring("w_codes", 4, [P, BANK], U32)
+        w_scales = ring("w_scales", 4, [P, BANK], U8)
+        biased = ring("biased", 5, [P, 2, 2, 2, HALF], F32)
+        cos_part = ring("cos_part", 3, [P, 2, 2, 2, HALF], F32)
+        sin_part = ring("sin_part", 3, [P, 2, 2, 2, HALF], F32)
+        results = ring("results", 10, [P, 2, 2, 2, HALF], F32)
+        turn_banks = banks("turn", 4)
+        free_acc = banks("acc", 3)
+        table = ps.tile([P, 2, 4, HALF], F32, name="table")
+
+        words = {}
+        sorted_of = {}
+        operand = {}
+        acc_of = {}
+
+        def load(n):
+            kind, a, kh = units[n]
+            if n in words:
+                return
+            span = 2 if n >= WIDE_FROM else 1
+            rows = x_rows[:, 2 * a : 2 * a + 2, :] if kind == "x" else w_rows(a)
+            raw = sb.tile([P, 2, span * UNIT_K], BF16, name="raw%d" % n, align_bytes=64)
+            nc.sync.dma_start(out=raw[:], in_=rows[:, :, kh * UNIT_K : (kh + span) * UNIT_K])
+            for d in range(span):
+                words[n + d] = raw[:].bitcast(F32)[:, :, d * 512 : (d + 1) * 512]
+
+        def sort_words(n):
+            dst = sorted_words[len(sorted_of) % len(sorted_words)]
+            sorted_of[n] = dst
+            if n in VECTOR_SORTED:
+                nc.vector.tensor_copy(out=dst[:], in_=words[n].rearrange("p r (g w u) -> p (r g) u w", g=2, u=2))
+            elif n < WIDE_FROM:
+                nc.scalar.copy(out=dst[:], in_=words[n].rearrange("p r (g w u) -> p (r g) u w", g=2, u=2))
+            else:
+                for r in range(2):
+                    nc.scalar.copy(out=dst[:, 2 * r : 2 * r + 2], in_=words[n][:, r, :].rearrange("p (g w u) -> p g u w", g=2, u=2))
+
+        def turn(n):
+            dst = grouped[n % len(grouped)][:].bitcast(F32).rearrange("p (g r c u) -> p g r c u", g=2, r=2, u=2)
+            for g in range(2):
+                bank = turn_banks[(2 * n + g) % len(turn_banks)][:].rearrange("p (r u c) -> p r u c", r=2, u=2)
+                for r in range(2):
+                    for u in range(2):
+                        if n in sorted_of:
+                            src = sorted_of[n][:, 2 * r + g, u, :]
+                        else:
+                            src = words[n][:, r, 256 * g + u : 256 * (g + 1) : 2]
+                        nc.tensor.transpose(bank[:, r, u, :], src, ident_f32[:])
+                nc.scalar.copy(out=dst[:, g], in_=bank.rearrange("p r u c -> p r c u"))
+
+        def quantize(n):
+            kind, a, kh = units[n]
+            codes, scales = (x_codes, x_scales) if kind == "x" else (w_codes, w_scales)
+            slot = (2 * a + kh) % len(codes)
+            nc.vector.quantize_mx(out=codes[slot][:].bitcast(E5M2X4), scales=scales[slot][:], in_=grouped[n % len(grouped)][:])
+            operand[(kind, slot)] = units[n]
+
+        def multiply(tile, kh):
+            q, jp = divmod(tile, 2)
+            if kh == 0:
+                acc_of[tile] = free_acc[0]
+                free_acc.remove(acc_of[tile])
+            xs, ws = 2 * jp + kh, (2 * q + kh) % len(w_codes)
+            assert operand[("x", xs)] == ("x", jp, kh) and operand[("w", ws)] == ("w", q, kh)
+            for jj in range(2):
+                for g in range(2):
+                    x_cols = slice((2 * g + jj) * P, (2 * g + jj + 1) * P)
+                    w_cols = slice(g * PAIR_ROWS, (g + 1) * PAIR_ROWS)
+                    nc.tensor.matmul_mx(
+                        out=acc_of[tile][:, jj * PAIR_ROWS : (jj + 1) * PAIR_ROWS],
+                        lhsT=x_codes[xs][:, x_cols].bitcast(E5M2X4),
+                        lhsT_scale=x_scales[xs][:, x_cols],
+                        rhs=w_codes[ws][:, w_cols].bitcast(E5M2X4),
+                        rhs_scale=w_scales[ws][:, w_cols],
+                        start=(kh == 0 and jj == 0 and g == 0),
+                        stop=(kh == 1 and jj == 1 and g == 1),
+                    )
+
+        def spread_bias(c):
+            bank = free_acc[0]
+            free_acc.remove(bank)
+            nc.tensor.matmul(bank[:], lhsT=ident_bf16[:, c : c + 1].to_broadcast([P, P]), rhs=bias_rows[:], start=True, stop=True)
+            nc.scalar.copy(out=bias[c][:].rearrange("p a n -> p (a n)"), in_=bank[:])
+            free_acc.append(bank)
+
+        def fill_table():
+            flat = "p a j d -> p (a j d)"
+            nc.tensor.matmul(table[:].rearrange(flat), lhsT=ident_bf16[:], rhs=cos_sin[:].rearrange(flat), start=True, stop=True)
+
+        def store(tile, src):
+            q, jp = divmod(tile, 2)
+            nc.sync.dma_start(out=out_rows(q)[:, :, 2 * jp : 2 * jp + 2, :], in_=src[:].rearrange("p h j a d -> p h j (a d)"))
+
+        def add_bias(tile):
+            q = tile // 2
+            acc = acc_of[tile][:].rearrange("p (j h d) -> p j h d", j=2, h=2)
+            row = bias[q // 2][:, q % 2 : q % 2 + 1, :].to_broadcast([P, 2, PAIR_ROWS]).rearrange("p j (h d) -> p j h d", h=2)
+            free_acc.append(acc_of[tile])
+            dst = biased[tile % len(biased)] if tile < ROPE_TILES else results[tile % len(results)]
+            nc.vector.tensor_tensor(out=dst[:].rearrange("p h j a d -> p j h (a d)"), in0=acc, in1=row, op=ADD)
+            if tile >= ROPE_TILES:
+                store(tile, dst)
+
+        def rotate(tile):
+            jp = tile % 2
+            t = biased[tile % len(biased)]
+            cp = cos_part[tile % len(cos_part)]
+            sp = sin_part[tile % len(sin_part)]
+            on_pool = POOL_COS_EVERY and tile % POOL_COS_EVERY == POOL_COS_EVERY - 1
+            engine, tab = (nc.gpsimd, cos_sin) if on_pool else (nc.vector, table)
+            by_token = "p h j a d -> p j h (a d)"
+            cos_f = tab[:, 0, 2 * jp : 2 * jp + 2, :].unsqueeze(2).to_broadcast([P, 2, 4, HALF])
+            engine.tensor_tensor(out=cp[:].rearrange(by_token), in0=t[:].rearrange(by_token), in1=cos_f, op=MULT)
+            sin_f = table[:, 1, 2 * jp : 2 * jp + 2, :].unsqueeze(1).to_broadcast([P, 2, 2, HALF])
+            nc.vector.scalar_tensor_tensor(out=sp[:, :, :, 0, :], in0=t[:, :, :, 1, :], scalar=-1.0, in1=sin_f, op0=MULT, op1=MULT)
+            nc.vector.tensor_tensor(out=sp[:, :, :, 1, :], in0=t[:, :, :, 0, :], in1=sin_f, op=MULT)
+
+        def combine(tile):
+            res = results[tile % len(results)]
+            engine = nc.gpsimd if POOL_ADD else nc.vector
+            flat = "p h j a d -> p (h j a d)"
+            engine.tensor_tensor(
+                out=res[:].rearrange(flat),
+                in0=cos_part[tile % len(cos_part)][:].rearrange(flat),
+                in1=sin_part[tile % len(sin_part)][:].rearrange(flat),
+                op=ADD,
+            )
+            store(tile, res)
+
+        nc.vector.memset(bias_rows[:].bitcast(U32), 0)
+        make_identity(nc, ident_bf16[:])
+        make_identity(nc, ident_f32[:])
+        load(0)
+        nc.sync.dma_start(out=bias_rows[0:4, :], in_=bq.rearrange("(c n) -> c n", n=BANK))
+        nc.sync.dma_start(out=bias_rows[4:6, :], in_=bkv.rearrange("(c n) -> c n", n=BANK))
+        load(1)
+        nc.sync.dma_start(out=cos_sin[:, 0], in_=cos.rearrange("(p j) d -> p j d", j=4))
+        nc.sync.dma_start(out=cos_sin[:, 1], in_=sin.rearrange("(p j) d -> p j d", j=4))
+        for n in range(2, LOAD_AHEAD):
+            load(n)
+        for c in range(EARLY_BIAS):
+            spread_bias(c)
+
+        plan = []
+
+        def at(key, fn, *args):
+            plan.append((key, len(plan), fn, args))
+
+        def turn_key(n):
+            if n < RUN_FROM:
+                return n + 0.9 - (HEAD_LEAD if n < LEAD_UNTIL else 2.0)
+            return n - n % 2 - 0.08
+
+        for n in range(len(units)):
+            if n >= LOAD_AHEAD:
+                at(n - LOAD_AHEAD - 2.5, load, n)
+            if n in VECTOR_SORTED:
+                at(turn_key(n) - 0.05, sort_words, n)
+            elif n >= SCALAR_SORT_FROM and n % 4 in SCALAR_SORTED:
+                at(max(turn_key(n - SORT_AHEAD), turn_key(min(n - 1, SORT_NOT_BEFORE))) + 0.01, sort_words, n)
+            at(turn_key(n), turn, n)
+            at(n + 0.9, quantize, n)
+        at(TABLE_KEY, fill_table)
+
+        def last_unit(tile, kh):
+            q, jp = divmod(tile, 2)
+            return max(units.index(("x", jp, kh)), units.index(("w", q, kh)))
+
+        bias_slot = {0: SLOT0, 1: SLOT1}
+        for tile in range(TILES):
+            for kh in range(2):
+                n = last_unit(tile, kh)
+                if last_unit(tile, 1) + 1 < RUN_FROM:
+                    at(n + 0.95, multiply, tile, kh)
+                else:
+                    at(last_unit(tile, 1) + 0.95, multiply, tile, kh)
+            slot = bias_slot.get(tile, tile + T_OFF)
+            at(slot + 0.1, add_bias, tile)
+            if tile < ROPE_TILES:
+                rslot = slot + (ROT_LAG if tile >= EARLY_ROT else 1) + (1 if tile >= LAG_STEP else 0)
+                at(rslot + 0.2, rotate, tile)
+                at(rslot + 0.3 if POOL_ADD else rslot + 1.15, combine, tile)
+        for c in range(EARLY_BIAS, PAIRS // 2):
+            at(4 * c + 1.91, spread_bias, c)
+        for key, order, fn, args in sorted(plan, key=lambda e: (e[0], e[1])):
+            fn(*args)

@@ -4,7 +4,10 @@ import concourse.mybir as mybir
 from concourse.masks import make_identity
 
 S, E, HD = 512, 2048, 128
-FLOPS = 2 * S * E * 3072
+PAIRS = 12
+Q_PAIRS = 8
+ROPE_PAIRS = 10
+FLOPS = 2 * S * E * PAIRS * 2 * HD
 
 F32 = mybir.dt.float32
 BF16 = mybir.dt.bfloat16
@@ -12,40 +15,22 @@ U32 = mybir.dt.uint32
 U8 = mybir.dt.uint8
 E5M2X4 = mybir.dt.float8_e5m2_x4
 ADD = mybir.AluOpType.add
-SUB = mybir.AluOpType.subtract
 MULT = mybir.AluOpType.mult
 
 P = 128
 HALF = HD // 2
 BANK = 512
-PAIRS = 12
-ROPE_PAIRS = 10
-Q_PAIRS = 8
+GROUPS = S // P
 PAIR_ROWS = 2 * HD
-UNIT_K = 1024
-TILES = 2 * PAIRS
+SLAB_K = E // 2
+PASS_WORDS = 256
 ROPE_TILES = 2 * ROPE_PAIRS
 
-VECTOR_SORTED = (0, 1, 2, 3, 4, 5, 6, 7)
-SCALAR_SORTED = (0, 1, 2)
-SCALAR_SORT_FROM = 10
+FIRST_LOADS = 16
+RAW_SLABS = FIRST_LOADS + 2
+TABLES_AFTER = 5
+VECTOR_SORTS = 8
 SORT_AHEAD = 4
-SORT_NOT_BEFORE = 9
-ROT_LAG = 1
-LAG_STEP = 99
-LOAD_AHEAD = 10
-POOL_ADD = True
-POOL_COS_EVERY = 0
-EARLY_BIAS = 2
-HEAD_LEAD = 3.0
-TABLE_KEY = -0.5
-LEAD_UNTIL = 12
-SLOT0 = 5
-SLOT1 = 7
-EARLY_ROT = 2
-RUN_FROM = 10
-T_OFF = 7
-WIDE_FROM = 99
 
 
 def tile_qwen2attention_pa_kernel(tc, x, Wq, bq, Wkv, bkv, cos, sin, out_0, out_1, out_2):
@@ -61,9 +46,9 @@ def tile_qwen2attention_pa_kernel(tc, x, Wq, bq, Wkv, bkv, cos, sin, out_0, out_
         def banks(name, count):
             return [ps.tile([P, BANK], F32, name="%s%d" % (name, i)) for i in range(count)]
 
-        units = [("x", 0, 0), ("w", 0, 0), ("x", 0, 1), ("w", 0, 1), ("x", 1, 0), ("x", 1, 1)]
-        units = units + [("w", q, kh) for q in range(1, PAIRS) for kh in range(2)]
-        x_rows = x[0].rearrange("(p j) k -> p j k", j=4)
+        slabs = [("x", 0, 0), ("w", 0, 0), ("x", 0, 1), ("w", 0, 1), ("x", 1, 0), ("x", 1, 1)]
+        slabs = slabs + [("w", q, kh) for q in range(1, PAIRS) for kh in range(2)]
+        x_rows = x[0].rearrange("(p j) k -> p j k", j=GROUPS)
 
         def w_rows(q):
             w, q0 = (Wq, q) if q < Q_PAIRS else (Wkv, q - Q_PAIRS)
@@ -71,56 +56,55 @@ def tile_qwen2attention_pa_kernel(tc, x, Wq, bq, Wkv, bkv, cos, sin, out_0, out_
 
         def out_rows(q):
             o, q0 = (out_0, q) if q < Q_PAIRS else (out_1, q - Q_PAIRS) if q < ROPE_PAIRS else (out_2, q - ROPE_PAIRS)
-            return o[0, 2 * q0 : 2 * q0 + 2].rearrange("h (p j) d -> p h j d", j=4)
+            return o[0, 2 * q0 : 2 * q0 + 2].rearrange("h (p j) d -> p h j d", j=GROUPS)
 
         ident_f32 = sb.tile([P, P], F32, name="ident_f32", align_bytes=64)
         ident_bf16 = sb.tile([P, P], BF16, name="ident_bf16", align_bytes=64)
         bias_rows = sb.tile([P, BANK], BF16, name="bias_rows", align_bytes=64)
-        cos_sin = sb.tile([P, 2, 4, HALF], BF16, name="cos_sin", align_bytes=64)
-        bias = ring("bias", PAIRS // 2, [P, 2, PAIR_ROWS], BF16)
+        cos_sin = sb.tile([P, 2, GROUPS, HALF], BF16, name="cos_sin", align_bytes=64)
+        bias = sb.tile([P, PAIRS, PAIR_ROWS], BF16, name="bias", align_bytes=64)
         sorted_words = ring("sorted", SORT_AHEAD, [P, 4, 2, P], F32)
-        grouped = ring("grouped", 4, [P, 4 * BANK], BF16)
+        raws = ring("raw", RAW_SLABS, [P, 2, SLAB_K], BF16)
+        packed = ring("packed", 4, [P, 2 * SLAB_K], BF16)
         x_codes = ring("x_codes", 4, [P, BANK], U32)
         x_scales = ring("x_scales", 4, [P, BANK], U8)
         w_codes = ring("w_codes", 4, [P, BANK], U32)
         w_scales = ring("w_scales", 4, [P, BANK], U8)
-        biased = ring("biased", 5, [P, 2, 2, 2, HALF], F32)
-        cos_part = ring("cos_part", 3, [P, 2, 2, 2, HALF], F32)
-        sin_part = ring("sin_part", 3, [P, 2, 2, 2, HALF], F32)
-        results = ring("results", 10, [P, 2, 2, 2, HALF], F32)
+        widths = (2, GROUPS)
+        biased = {n: ring("biased%d_" % n, 2, [P, 2, n, 2, HALF], F32) for n in widths}
+        cos_term = {n: ring("cos_term%d_" % n, 2, [P, 2, n, 2, HALF], F32) for n in widths}
+        sin_term = {n: ring("sin_term%d_" % n, 2, [P, 2, n, 2, HALF], F32) for n in widths}
+        tile_results = ring("tile_result", 8, [P, 2, 2, 2, HALF], F32)
+        pair_results = ring("pair_result", 4, [P, 2, GROUPS, 2, HALF], F32)
         turn_banks = banks("turn", 4)
-        free_acc = banks("acc", 3)
-        table = ps.tile([P, 2, 4, HALF], F32, name="table")
+        free_banks = banks("acc", 3)
+        table = ps.tile([P, 2, GROUPS, HALF], F32, name="table")
 
-        words = {}
         sorted_of = {}
-        operand = {}
-        acc_of = {}
+        bank_of = {}
+
+        def take_bank():
+            bank = free_banks[0]
+            free_banks.remove(bank)
+            return bank
 
         def load(n):
-            kind, a, kh = units[n]
-            if n in words:
-                return
-            span = 2 if n >= WIDE_FROM else 1
-            rows = x_rows[:, 2 * a : 2 * a + 2, :] if kind == "x" else w_rows(a)
-            raw = sb.tile([P, 2, span * UNIT_K], BF16, name="raw%d" % n, align_bytes=64)
-            nc.sync.dma_start(out=raw[:], in_=rows[:, :, kh * UNIT_K : (kh + span) * UNIT_K])
-            for d in range(span):
-                words[n + d] = raw[:].bitcast(F32)[:, :, d * 512 : (d + 1) * 512]
+            operand, block, kh = slabs[n]
+            rows = x_rows[:, 2 * block : 2 * block + 2, :] if operand == "x" else w_rows(block)
+            nc.sync.dma_start(out=raws[n % RAW_SLABS][:], in_=rows[:, :, kh * SLAB_K : (kh + 1) * SLAB_K])
 
         def sort_words(n):
-            dst = sorted_words[len(sorted_of) % len(sorted_words)]
+            dst = sorted_words[len(sorted_of) % SORT_AHEAD]
             sorted_of[n] = dst
-            if n in VECTOR_SORTED:
-                nc.vector.tensor_copy(out=dst[:], in_=words[n].rearrange("p r (g w u) -> p (r g) u w", g=2, u=2))
-            elif n < WIDE_FROM:
-                nc.scalar.copy(out=dst[:], in_=words[n].rearrange("p r (g w u) -> p (r g) u w", g=2, u=2))
+            src = raws[n % RAW_SLABS][:].bitcast(F32).rearrange("p r (g w u) -> p (r g) u w", g=2, u=2)
+            if n < VECTOR_SORTS:
+                nc.vector.tensor_copy(out=dst[:], in_=src)
             else:
-                for r in range(2):
-                    nc.scalar.copy(out=dst[:, 2 * r : 2 * r + 2], in_=words[n][:, r, :].rearrange("p (g w u) -> p g u w", g=2, u=2))
+                nc.scalar.copy(out=dst[:], in_=src)
 
         def turn(n):
-            dst = grouped[n % len(grouped)][:].bitcast(F32).rearrange("p (g r c u) -> p g r c u", g=2, r=2, u=2)
+            words = raws[n % RAW_SLABS][:].bitcast(F32)
+            dst = packed[n % len(packed)][:].bitcast(F32).rearrange("p (g r c u) -> p g r c u", g=2, r=2, u=2)
             for g in range(2):
                 bank = turn_banks[(2 * n + g) % len(turn_banks)][:].rearrange("p (r u c) -> p r u c", r=2, u=2)
                 for r in range(2):
@@ -128,143 +112,229 @@ def tile_qwen2attention_pa_kernel(tc, x, Wq, bq, Wkv, bkv, cos, sin, out_0, out_
                         if n in sorted_of:
                             src = sorted_of[n][:, 2 * r + g, u, :]
                         else:
-                            src = words[n][:, r, 256 * g + u : 256 * (g + 1) : 2]
+                            src = words[:, r, PASS_WORDS * g + u : PASS_WORDS * (g + 1) : 2]
                         nc.tensor.transpose(bank[:, r, u, :], src, ident_f32[:])
                 nc.scalar.copy(out=dst[:, g], in_=bank.rearrange("p r u c -> p r c u"))
 
         def quantize(n):
-            kind, a, kh = units[n]
-            codes, scales = (x_codes, x_scales) if kind == "x" else (w_codes, w_scales)
-            slot = (2 * a + kh) % len(codes)
-            nc.vector.quantize_mx(out=codes[slot][:].bitcast(E5M2X4), scales=scales[slot][:], in_=grouped[n % len(grouped)][:])
-            operand[(kind, slot)] = units[n]
+            operand, block, kh = slabs[n]
+            codes, scales = (x_codes, x_scales) if operand == "x" else (w_codes, w_scales)
+            slot = (2 * block + kh) % len(codes)
+            nc.vector.quantize_mx(out=codes[slot][:].bitcast(E5M2X4), scales=scales[slot][:], in_=packed[n % len(packed)][:])
 
         def multiply(tile, kh):
-            q, jp = divmod(tile, 2)
+            q, a = divmod(tile, 2)
             if kh == 0:
-                acc_of[tile] = free_acc[0]
-                free_acc.remove(acc_of[tile])
-            xs, ws = 2 * jp + kh, (2 * q + kh) % len(w_codes)
-            assert operand[("x", xs)] == ("x", jp, kh) and operand[("w", ws)] == ("w", q, kh)
-            for jj in range(2):
+                bank_of[tile] = take_bank()
+            x_slot, w_slot = 2 * a + kh, (2 * q + kh) % len(w_codes)
+            for r in range(2):
                 for g in range(2):
-                    x_cols = slice((2 * g + jj) * P, (2 * g + jj + 1) * P)
+                    x_cols = slice((2 * g + r) * P, (2 * g + r + 1) * P)
                     w_cols = slice(g * PAIR_ROWS, (g + 1) * PAIR_ROWS)
                     nc.tensor.matmul_mx(
-                        out=acc_of[tile][:, jj * PAIR_ROWS : (jj + 1) * PAIR_ROWS],
-                        lhsT=x_codes[xs][:, x_cols].bitcast(E5M2X4),
-                        lhsT_scale=x_scales[xs][:, x_cols],
-                        rhs=w_codes[ws][:, w_cols].bitcast(E5M2X4),
-                        rhs_scale=w_scales[ws][:, w_cols],
-                        start=(kh == 0 and jj == 0 and g == 0),
-                        stop=(kh == 1 and jj == 1 and g == 1),
+                        out=bank_of[tile][:, r * PAIR_ROWS : (r + 1) * PAIR_ROWS],
+                        lhsT=x_codes[x_slot][:, x_cols].bitcast(E5M2X4),
+                        lhsT_scale=x_scales[x_slot][:, x_cols],
+                        rhs=w_codes[w_slot][:, w_cols].bitcast(E5M2X4),
+                        rhs_scale=w_scales[w_slot][:, w_cols],
+                        start=(kh == 0 and r == 0 and g == 0),
+                        stop=(kh == 1 and r == 1 and g == 1),
                     )
 
-        def spread_bias(c):
-            bank = free_acc[0]
-            free_acc.remove(bank)
-            nc.tensor.matmul(bank[:], lhsT=ident_bf16[:, c : c + 1].to_broadcast([P, P]), rhs=bias_rows[:], start=True, stop=True)
-            nc.scalar.copy(out=bias[c][:].rearrange("p a n -> p (a n)"), in_=bank[:])
-            free_acc.append(bank)
+        def spread_bias(m):
+            bank = take_bank()
+            two_rows = bank[:].bitcast(BF16)
+            for d in range(2):
+                c = 2 * m + d
+                nc.tensor.matmul(
+                    two_rows[:, d * BANK : (d + 1) * BANK],
+                    lhsT=ident_bf16[:, c : c + 1].to_broadcast([P, P]),
+                    rhs=bias_rows[:],
+                    start=True,
+                    stop=True,
+                )
+            nc.scalar.copy(out=bias[:, 4 * m : 4 * m + 4, :].rearrange("p q n -> p (q n)"), in_=two_rows)
+            free_banks.append(bank)
 
         def fill_table():
-            flat = "p a j d -> p (a j d)"
+            flat = "p f j d -> p (f j d)"
             nc.tensor.matmul(table[:].rearrange(flat), lhsT=ident_bf16[:], rhs=cos_sin[:].rearrange(flat), start=True, stop=True)
 
-        def store(tile, src):
-            q, jp = divmod(tile, 2)
-            nc.sync.dma_start(out=out_rows(q)[:, :, 2 * jp : 2 * jp + 2, :], in_=src[:].rearrange("p h j a d -> p h j (a d)"))
+        def span(tile):
+            return (2 * tile, 2) if tile < 2 else (0, GROUPS)
+
+        def values(rings, tile):
+            width = span(tile)[1]
+            return rings[width][(tile if tile < 2 else tile // 2) % 2]
+
+        def tile_result(tile):
+            return tile_results[tile % len(tile_results)][:]
+
+        def store(q, j0, src):
+            nc.sync.dma_start(
+                out=out_rows(q)[:, :, j0 : j0 + src.shape[2], :], in_=src.rearrange("p h j a d -> p h j (a d)")
+            )
 
         def add_bias(tile):
-            q = tile // 2
-            acc = acc_of[tile][:].rearrange("p (j h d) -> p j h d", j=2, h=2)
-            row = bias[q // 2][:, q % 2 : q % 2 + 1, :].to_broadcast([P, 2, PAIR_ROWS]).rearrange("p j (h d) -> p j h d", h=2)
-            free_acc.append(acc_of[tile])
-            dst = biased[tile % len(biased)] if tile < ROPE_TILES else results[tile % len(results)]
-            nc.vector.tensor_tensor(out=dst[:].rearrange("p h j a d -> p j h (a d)"), in0=acc, in1=row, op=ADD)
+            q, a = divmod(tile, 2)
+            sums = bank_of[tile][:].rearrange("p (j h d) -> p j h d", j=2, h=2)
+            row = bias[:, q : q + 1, :].to_broadcast([P, 2, PAIR_ROWS]).rearrange("p j (h d) -> p j h d", h=2)
+            j = 2 * a - span(tile)[0]
+            dst = values(biased, tile)[:, :, j : j + 2] if tile < ROPE_TILES else tile_result(tile)
+            nc.vector.tensor_tensor(out=dst.rearrange("p h j a d -> p j h (a d)"), in0=sums, in1=row, op=ADD)
+            free_banks.append(bank_of[tile])
             if tile >= ROPE_TILES:
-                store(tile, dst)
+                store(q, 2 * a, dst)
+
+        def sin_factor(tile, heads):
+            j0, width = span(tile)
+            return table[:, 1, j0 : j0 + width, :].unsqueeze(1).to_broadcast([P, heads, width, HALF])
+
+        def upper_sin_term(tile, h):
+            nc.vector.tensor_tensor(
+                out=values(sin_term, tile)[:, h : h + 1, :, 1, :],
+                in0=values(biased, tile)[:, h : h + 1, :, 0, :],
+                in1=sin_factor(tile, 1),
+                op=MULT,
+            )
 
         def rotate(tile):
-            jp = tile % 2
-            t = biased[tile % len(biased)]
-            cp = cos_part[tile % len(cos_part)]
-            sp = sin_part[tile % len(sin_part)]
-            on_pool = POOL_COS_EVERY and tile % POOL_COS_EVERY == POOL_COS_EVERY - 1
-            engine, tab = (nc.gpsimd, cos_sin) if on_pool else (nc.vector, table)
-            by_token = "p h j a d -> p j h (a d)"
-            cos_f = tab[:, 0, 2 * jp : 2 * jp + 2, :].unsqueeze(2).to_broadcast([P, 2, 4, HALF])
-            engine.tensor_tensor(out=cp[:].rearrange(by_token), in0=t[:].rearrange(by_token), in1=cos_f, op=MULT)
-            sin_f = table[:, 1, 2 * jp : 2 * jp + 2, :].unsqueeze(1).to_broadcast([P, 2, 2, HALF])
-            nc.vector.scalar_tensor_tensor(out=sp[:, :, :, 0, :], in0=t[:, :, :, 1, :], scalar=-1.0, in1=sin_f, op0=MULT, op1=MULT)
-            nc.vector.tensor_tensor(out=sp[:, :, :, 1, :], in0=t[:, :, :, 0, :], in1=sin_f, op=MULT)
+            j0, width = span(tile)
+            t = values(biased, tile)
+            by_group = "p h j a d -> p j h (a d)"
+            nc.vector.tensor_tensor(
+                out=values(cos_term, tile)[:].rearrange(by_group),
+                in0=t[:].rearrange(by_group),
+                in1=table[:, 0, j0 : j0 + width, :].unsqueeze(2).to_broadcast([P, width, 4, HALF]),
+                op=MULT,
+            )
+            nc.vector.scalar_tensor_tensor(
+                out=values(sin_term, tile)[:, :, :, 0, :],
+                in0=t[:, :, :, 1, :],
+                scalar=-1.0,
+                in1=sin_factor(tile, 2),
+                op0=MULT,
+                op1=MULT,
+            )
+            upper_sin_term(tile, 0)
 
-        def combine(tile):
-            res = results[tile % len(results)]
-            engine = nc.gpsimd if POOL_ADD else nc.vector
-            flat = "p h j a d -> p (h j a d)"
+        def add_terms(engine, tile, lo, result):
+            hi = lo + result.shape[2]
+            rows = "p h j a d -> p h (j a d)"
             engine.tensor_tensor(
-                out=res[:].rearrange(flat),
-                in0=cos_part[tile % len(cos_part)][:].rearrange(flat),
-                in1=sin_part[tile % len(sin_part)][:].rearrange(flat),
+                out=result.rearrange(rows),
+                in0=values(cos_term, tile)[:, :, lo:hi].rearrange(rows),
+                in1=values(sin_term, tile)[:, :, lo:hi].rearrange(rows),
                 op=ADD,
             )
-            store(tile, res)
+            store(tile // 2, span(tile)[0] + lo, result)
+
+        def finish(tile):
+            upper_sin_term(tile, 1)
+            result = tile_result(tile) if tile < 2 else pair_results[tile // 2 % len(pair_results)][:]
+            add_terms(nc.gpsimd, tile, 0, result)
+
+        def sort_and_turn(n):
+            sort_words(n)
+            turn(n)
 
         nc.vector.memset(bias_rows[:].bitcast(U32), 0)
         make_identity(nc, ident_bf16[:])
         make_identity(nc, ident_f32[:])
+        q_bias_rows = Q_PAIRS // 2
         load(0)
-        nc.sync.dma_start(out=bias_rows[0:4, :], in_=bq.rearrange("(c n) -> c n", n=BANK))
-        nc.sync.dma_start(out=bias_rows[4:6, :], in_=bkv.rearrange("(c n) -> c n", n=BANK))
-        load(1)
-        nc.sync.dma_start(out=cos_sin[:, 0], in_=cos.rearrange("(p j) d -> p j d", j=4))
-        nc.sync.dma_start(out=cos_sin[:, 1], in_=sin.rearrange("(p j) d -> p j d", j=4))
-        for n in range(2, LOAD_AHEAD):
+        nc.sync.dma_start(out=bias_rows[0:q_bias_rows, :], in_=bq.rearrange("(c n) -> c n", n=BANK))
+        nc.sync.dma_start(out=bias_rows[q_bias_rows : PAIRS // 2, :], in_=bkv.rearrange("(c n) -> c n", n=BANK))
+        for n in range(1, FIRST_LOADS):
             load(n)
-        for c in range(EARLY_BIAS):
-            spread_bias(c)
+            if n == TABLES_AFTER:
+                nc.sync.dma_start(out=cos_sin[:, 0], in_=cos.rearrange("(p j) d -> p j d", j=GROUPS))
+                nc.sync.dma_start(out=cos_sin[:, 1], in_=sin.rearrange("(p j) d -> p j d", j=GROUPS))
 
-        plan = []
+        spread_bias(0)
+        sort_and_turn(0)
+        sort_and_turn(1)
+        spread_bias(1)
+        sort_and_turn(2)
+        quantize(0)
+        sort_and_turn(3)
+        quantize(1)
+        multiply(0, 0)
+        sort_and_turn(4)
+        quantize(2)
+        sort_and_turn(5)
+        quantize(3)
+        multiply(0, 1)
+        sort_and_turn(6)
+        quantize(4)
+        sort_words(8)
+        multiply(1, 0)
+        add_bias(0)
+        fill_table()
+        sort_and_turn(7)
+        quantize(5)
+        multiply(1, 1)
+        rotate(0)
+        turn(8)
+        quantize(6)
+        turn(9)
+        add_bias(1)
+        multiply(2, 0)
+        multiply(3, 0)
+        load(FIRST_LOADS)
+        load(FIRST_LOADS + 1)
+        quantize(7)
+        rotate(1)
+        multiply(2, 1)
+        multiply(3, 1)
+        sort_words(10)
+        quantize(8)
+        sort_words(11)
+        quantize(9)
+        finish(0)
+        sort_words(12)
+        multiply(4, 0)
+        multiply(4, 1)
+        turn(10)
+        turn(11)
+        sort_words(14)
+        add_bias(2)
+        add_bias(3)
+        multiply(5, 0)
+        multiply(5, 1)
+        finish(1)
+        rotate(2)
 
-        def at(key, fn, *args):
-            plan.append((key, len(plan), fn, args))
-
-        def turn_key(n):
-            if n < RUN_FROM:
-                return n + 0.9 - (HEAD_LEAD if n < LEAD_UNTIL else 2.0)
-            return n - n % 2 - 0.08
-
-        for n in range(len(units)):
-            if n >= LOAD_AHEAD:
-                at(n - LOAD_AHEAD - 2.5, load, n)
-            if n in VECTOR_SORTED:
-                at(turn_key(n) - 0.05, sort_words, n)
-            elif n >= SCALAR_SORT_FROM and n % 4 in SCALAR_SORTED:
-                at(max(turn_key(n - SORT_AHEAD), turn_key(min(n - 1, SORT_NOT_BEFORE))) + 0.01, sort_words, n)
-            at(turn_key(n), turn, n)
-            at(n + 0.9, quantize, n)
-        at(TABLE_KEY, fill_table)
-
-        def last_unit(tile, kh):
-            q, jp = divmod(tile, 2)
-            return max(units.index(("x", jp, kh)), units.index(("w", q, kh)))
-
-        bias_slot = {0: SLOT0, 1: SLOT1}
-        for tile in range(TILES):
+        for q in range(2, ROPE_PAIRS):
+            for n in range(FIRST_LOADS + 2 * q - 2, min(FIRST_LOADS + 2 * q, len(slabs))):
+                load(n)
+            if q == Q_PAIRS - 2:
+                spread_bias(2)
+            lead = 2 * (q + 2) + 4
+            turn(lead)
+            turn(lead + 1)
+            if lead + SORT_AHEAD < len(slabs):
+                sort_words(lead + SORT_AHEAD)
+            add_bias(2 * q)
+            add_bias(2 * q + 1)
+            quantize(lead - 2)
+            quantize(lead - 1)
             for kh in range(2):
-                n = last_unit(tile, kh)
-                if last_unit(tile, 1) + 1 < RUN_FROM:
-                    at(n + 0.95, multiply, tile, kh)
-                else:
-                    at(last_unit(tile, 1) + 0.95, multiply, tile, kh)
-            slot = bias_slot.get(tile, tile + T_OFF)
-            at(slot + 0.1, add_bias, tile)
-            if tile < ROPE_TILES:
-                rslot = slot + (ROT_LAG if tile >= EARLY_ROT else 1) + (1 if tile >= LAG_STEP else 0)
-                at(rslot + 0.2, rotate, tile)
-                at(rslot + 0.3 if POOL_ADD else rslot + 1.15, combine, tile)
-        for c in range(EARLY_BIAS, PAIRS // 2):
-            at(4 * c + 1.91, spread_bias, c)
-        for key, order, fn, args in sorted(plan, key=lambda e: (e[0], e[1])):
-            fn(*args)
+                multiply(2 * q + 2, kh)
+                multiply(2 * q + 3, kh)
+            finish(2 * q - 2)
+            rotate(2 * q)
+
+        last_keys, first_values = ROPE_TILES - 2, ROPE_TILES
+        upper_sin_term(last_keys, 1)
+        add_bias(first_values)
+        quantize(len(slabs) - 2)
+        quantize(len(slabs) - 1)
+        for kh in range(2):
+            multiply(first_values + 2, kh)
+            multiply(first_values + 3, kh)
+        add_terms(nc.vector, last_keys, 0, tile_result(last_keys))
+        add_bias(first_values + 1)
+        add_terms(nc.vector, last_keys, 2, tile_result(last_keys + 1))
+        add_bias(first_values + 2)
+        add_bias(first_values + 3)

from contextlib import ExitStack

import concourse.mybir as mybir
from concourse.masks import make_identity

S, E, HD = 512, 2048, 128
PAIRS = 12
Q_PAIRS = 8
ROPE_PAIRS = 10
FLOPS = 2 * S * E * PAIRS * 2 * HD

F32 = mybir.dt.float32
BF16 = mybir.dt.bfloat16
U32 = mybir.dt.uint32
U8 = mybir.dt.uint8
E5M2X4 = mybir.dt.float8_e5m2_x4
ADD = mybir.AluOpType.add
MULT = mybir.AluOpType.mult

P = 128
HALF = HD // 2
BANK = 512
GROUPS = S // P
PAIR_ROWS = 2 * HD
SLAB_K = E // 2
PASS_WORDS = 256
ROPE_TILES = 2 * ROPE_PAIRS

FIRST_LOADS = 16
RAW_SLABS = FIRST_LOADS + 2
TABLES_AFTER = 5
VECTOR_SORTS = 8
SORT_AHEAD = 4


def tile_qwen2attention_pa_kernel(tc, x, Wq, bq, Wkv, bkv, cos, sin, out_0, out_1, out_2):
    nc = tc.nc
    with ExitStack() as ctx:
        sb = ctx.enter_context(tc.tile_pool(name="sb", bufs=1))
        ps = ctx.enter_context(tc.psum_pool(name="ps", bufs=1))
        ctx.enter_context(tc.manual_schedule())

        def ring(name, count, shape, dtype):
            return [sb.tile(shape, dtype, name="%s%d" % (name, i), align_bytes=64) for i in range(count)]

        def banks(name, count):
            return [ps.tile([P, BANK], F32, name="%s%d" % (name, i)) for i in range(count)]

        slabs = [("x", 0, 0), ("w", 0, 0), ("x", 0, 1), ("w", 0, 1), ("x", 1, 0), ("x", 1, 1)]
        slabs = slabs + [("w", q, kh) for q in range(1, PAIRS) for kh in range(2)]
        x_rows = x[0].rearrange("(p j) k -> p j k", j=GROUPS)

        def w_rows(q):
            w, q0 = (Wq, q) if q < Q_PAIRS else (Wkv, q - Q_PAIRS)
            return w[q0 * PAIR_ROWS : (q0 + 1) * PAIR_ROWS, :].rearrange("(r p) k -> p r k", p=P)

        def out_rows(q):
            o, q0 = (out_0, q) if q < Q_PAIRS else (out_1, q - Q_PAIRS) if q < ROPE_PAIRS else (out_2, q - ROPE_PAIRS)
            return o[0, 2 * q0 : 2 * q0 + 2].rearrange("h (p j) d -> p h j d", j=GROUPS)

        ident_f32 = sb.tile([P, P], F32, name="ident_f32", align_bytes=64)
        ident_bf16 = sb.tile([P, P], BF16, name="ident_bf16", align_bytes=64)
        bias_rows = sb.tile([P, BANK], BF16, name="bias_rows", align_bytes=64)
        cos_sin = sb.tile([P, 2, GROUPS, HALF], BF16, name="cos_sin", align_bytes=64)
        bias = sb.tile([P, PAIRS, PAIR_ROWS], BF16, name="bias", align_bytes=64)
        sorted_words = ring("sorted", SORT_AHEAD, [P, 4, 2, P], F32)
        raws = ring("raw", RAW_SLABS, [P, 2, SLAB_K], BF16)
        packed = ring("packed", 4, [P, 2 * SLAB_K], BF16)
        x_codes = ring("x_codes", 4, [P, BANK], U32)
        x_scales = ring("x_scales", 4, [P, BANK], U8)
        w_codes = ring("w_codes", 4, [P, BANK], U32)
        w_scales = ring("w_scales", 4, [P, BANK], U8)
        widths = (2, GROUPS)
        biased = {n: ring("biased%d_" % n, 2, [P, 2, n, 2, HALF], F32) for n in widths}
        cos_term = {n: ring("cos_term%d_" % n, 2, [P, 2, n, 2, HALF], F32) for n in widths}
        sin_term = {n: ring("sin_term%d_" % n, 2, [P, 2, n, 2, HALF], F32) for n in widths}
        tile_results = ring("tile_result", 8, [P, 2, 2, 2, HALF], F32)
        pair_results = ring("pair_result", 4, [P, 2, GROUPS, 2, HALF], F32)
        turn_banks = banks("turn", 4)
        free_banks = banks("acc", 3)
        table = ps.tile([P, 2, GROUPS, HALF], F32, name="table")

        sorted_of = {}
        bank_of = {}

        def take_bank():
            bank = free_banks[0]
            free_banks.remove(bank)
            return bank

        def load(n):
            operand, block, kh = slabs[n]
            rows = x_rows[:, 2 * block : 2 * block + 2, :] if operand == "x" else w_rows(block)
            nc.sync.dma_start(out=raws[n % RAW_SLABS][:], in_=rows[:, :, kh * SLAB_K : (kh + 1) * SLAB_K])

        def sort_words(n):
            dst = sorted_words[len(sorted_of) % SORT_AHEAD]
            sorted_of[n] = dst
            src = raws[n % RAW_SLABS][:].bitcast(F32).rearrange("p r (g w u) -> p (r g) u w", g=2, u=2)
            if n < VECTOR_SORTS:
                nc.vector.tensor_copy(out=dst[:], in_=src)
            else:
                nc.scalar.copy(out=dst[:], in_=src)

        def turn(n):
            words = raws[n % RAW_SLABS][:].bitcast(F32)
            dst = packed[n % len(packed)][:].bitcast(F32).rearrange("p (g r c u) -> p g r c u", g=2, r=2, u=2)
            for g in range(2):
                bank = turn_banks[(2 * n + g) % len(turn_banks)][:].rearrange("p (r u c) -> p r u c", r=2, u=2)
                for r in range(2):
                    for u in range(2):
                        if n in sorted_of:
                            src = sorted_of[n][:, 2 * r + g, u, :]
                        else:
                            src = words[:, r, PASS_WORDS * g + u : PASS_WORDS * (g + 1) : 2]
                        nc.tensor.transpose(bank[:, r, u, :], src, ident_f32[:])
                nc.scalar.copy(out=dst[:, g], in_=bank.rearrange("p r u c -> p r c u"))

        def quantize(n):
            operand, block, kh = slabs[n]
            codes, scales = (x_codes, x_scales) if operand == "x" else (w_codes, w_scales)
            slot = (2 * block + kh) % len(codes)
            nc.vector.quantize_mx(out=codes[slot][:].bitcast(E5M2X4), scales=scales[slot][:], in_=packed[n % len(packed)][:])

        def multiply(tile, kh):
            q, a = divmod(tile, 2)
            if kh == 0:
                bank_of[tile] = take_bank()
            x_slot, w_slot = 2 * a + kh, (2 * q + kh) % len(w_codes)
            for r in range(2):
                for g in range(2):
                    x_cols = slice((2 * g + r) * P, (2 * g + r + 1) * P)
                    w_cols = slice(g * PAIR_ROWS, (g + 1) * PAIR_ROWS)
                    nc.tensor.matmul_mx(
                        out=bank_of[tile][:, r * PAIR_ROWS : (r + 1) * PAIR_ROWS],
                        lhsT=x_codes[x_slot][:, x_cols].bitcast(E5M2X4),
                        lhsT_scale=x_scales[x_slot][:, x_cols],
                        rhs=w_codes[w_slot][:, w_cols].bitcast(E5M2X4),
                        rhs_scale=w_scales[w_slot][:, w_cols],
                        start=(kh == 0 and r == 0 and g == 0),
                        stop=(kh == 1 and r == 1 and g == 1),
                    )

        def spread_bias(m):
            bank = take_bank()
            two_rows = bank[:].bitcast(BF16)
            for d in range(2):
                c = 2 * m + d
                nc.tensor.matmul(
                    two_rows[:, d * BANK : (d + 1) * BANK],
                    lhsT=ident_bf16[:, c : c + 1].to_broadcast([P, P]),
                    rhs=bias_rows[:],
                    start=True,
                    stop=True,
                )
            nc.scalar.copy(out=bias[:, 4 * m : 4 * m + 4, :].rearrange("p q n -> p (q n)"), in_=two_rows)
            free_banks.append(bank)

        def fill_table():
            flat = "p f j d -> p (f j d)"
            nc.tensor.matmul(table[:].rearrange(flat), lhsT=ident_bf16[:], rhs=cos_sin[:].rearrange(flat), start=True, stop=True)

        def span(tile):
            return (2 * tile, 2) if tile < 2 else (0, GROUPS)

        def values(rings, tile):
            width = span(tile)[1]
            return rings[width][(tile if tile < 2 else tile // 2) % 2]

        def tile_result(tile):
            return tile_results[tile % len(tile_results)][:]

        def store(q, j0, src):
            nc.sync.dma_start(
                out=out_rows(q)[:, :, j0 : j0 + src.shape[2], :], in_=src.rearrange("p h j a d -> p h j (a d)")
            )

        def add_bias(tile):
            q, a = divmod(tile, 2)
            sums = bank_of[tile][:].rearrange("p (j h d) -> p j h d", j=2, h=2)
            row = bias[:, q : q + 1, :].to_broadcast([P, 2, PAIR_ROWS]).rearrange("p j (h d) -> p j h d", h=2)
            j = 2 * a - span(tile)[0]
            dst = values(biased, tile)[:, :, j : j + 2] if tile < ROPE_TILES else tile_result(tile)
            nc.vector.tensor_tensor(out=dst.rearrange("p h j a d -> p j h (a d)"), in0=sums, in1=row, op=ADD)
            free_banks.append(bank_of[tile])
            if tile >= ROPE_TILES:
                store(q, 2 * a, dst)

        def sin_factor(tile, heads):
            j0, width = span(tile)
            return table[:, 1, j0 : j0 + width, :].unsqueeze(1).to_broadcast([P, heads, width, HALF])

        def upper_sin_term(tile, h):
            nc.vector.tensor_tensor(
                out=values(sin_term, tile)[:, h : h + 1, :, 1, :],
                in0=values(biased, tile)[:, h : h + 1, :, 0, :],
                in1=sin_factor(tile, 1),
                op=MULT,
            )

        def rotate(tile):
            j0, width = span(tile)
            t = values(biased, tile)
            by_group = "p h j a d -> p j h (a d)"
            nc.vector.tensor_tensor(
                out=values(cos_term, tile)[:].rearrange(by_group),
                in0=t[:].rearrange(by_group),
                in1=table[:, 0, j0 : j0 + width, :].unsqueeze(2).to_broadcast([P, width, 4, HALF]),
                op=MULT,
            )
            nc.vector.scalar_tensor_tensor(
                out=values(sin_term, tile)[:, :, :, 0, :],
                in0=t[:, :, :, 1, :],
                scalar=-1.0,
                in1=sin_factor(tile, 2),
                op0=MULT,
                op1=MULT,
            )
            upper_sin_term(tile, 0)

        def add_terms(engine, tile, lo, result):
            hi = lo + result.shape[2]
            rows = "p h j a d -> p h (j a d)"
            engine.tensor_tensor(
                out=result.rearrange(rows),
                in0=values(cos_term, tile)[:, :, lo:hi].rearrange(rows),
                in1=values(sin_term, tile)[:, :, lo:hi].rearrange(rows),
                op=ADD,
            )
            store(tile // 2, span(tile)[0] + lo, result)

        def finish(tile):
            upper_sin_term(tile, 1)
            result = tile_result(tile) if tile < 2 else pair_results[tile // 2 % len(pair_results)][:]
            add_terms(nc.gpsimd, tile, 0, result)

        def sort_and_turn(n):
            sort_words(n)
            turn(n)

        nc.vector.memset(bias_rows[:].bitcast(U32), 0)
        make_identity(nc, ident_bf16[:])
        make_identity(nc, ident_f32[:])
        q_bias_rows = Q_PAIRS // 2
        load(0)
        nc.sync.dma_start(out=bias_rows[0:q_bias_rows, :], in_=bq.rearrange("(c n) -> c n", n=BANK))
        nc.sync.dma_start(out=bias_rows[q_bias_rows : PAIRS // 2, :], in_=bkv.rearrange("(c n) -> c n", n=BANK))
        for n in range(1, FIRST_LOADS):
            load(n)
            if n == TABLES_AFTER:
                nc.sync.dma_start(out=cos_sin[:, 0], in_=cos.rearrange("(p j) d -> p j d", j=GROUPS))
                nc.sync.dma_start(out=cos_sin[:, 1], in_=sin.rearrange("(p j) d -> p j d", j=GROUPS))

        spread_bias(0)
        sort_and_turn(0)
        sort_and_turn(1)
        spread_bias(1)
        sort_and_turn(2)
        quantize(0)
        sort_and_turn(3)
        quantize(1)
        multiply(0, 0)
        sort_and_turn(4)
        quantize(2)
        sort_and_turn(5)
        quantize(3)
        multiply(0, 1)
        sort_and_turn(6)
        quantize(4)
        sort_words(8)
        multiply(1, 0)
        add_bias(0)
        fill_table()
        sort_and_turn(7)
        quantize(5)
        multiply(1, 1)
        rotate(0)
        turn(8)
        quantize(6)
        turn(9)
        add_bias(1)
        multiply(2, 0)
        multiply(3, 0)
        load(FIRST_LOADS)
        load(FIRST_LOADS + 1)
        quantize(7)
        rotate(1)
        multiply(2, 1)
        multiply(3, 1)
        sort_words(10)
        quantize(8)
        sort_words(11)
        quantize(9)
        finish(0)
        sort_words(12)
        multiply(4, 0)
        multiply(4, 1)
        turn(10)
        turn(11)
        sort_words(14)
        add_bias(2)
        add_bias(3)
        multiply(5, 0)
        multiply(5, 1)
        finish(1)
        rotate(2)

        for q in range(2, ROPE_PAIRS):
            for n in range(FIRST_LOADS + 2 * q - 2, min(FIRST_LOADS + 2 * q, len(slabs))):
                load(n)
            if q == Q_PAIRS - 2:
                spread_bias(2)
            lead = 2 * (q + 2) + 4
            turn(lead)
            turn(lead + 1)
            if lead + SORT_AHEAD < len(slabs):
                sort_words(lead + SORT_AHEAD)
            add_bias(2 * q)
            add_bias(2 * q + 1)
            quantize(lead - 2)
            quantize(lead - 1)
            for kh in range(2):
                multiply(2 * q + 2, kh)
                multiply(2 * q + 3, kh)
            finish(2 * q - 2)
            rotate(2 * q)

        last_keys, first_values = ROPE_TILES - 2, ROPE_TILES
        upper_sin_term(last_keys, 1)
        add_bias(first_values)
        quantize(len(slabs) - 2)
        quantize(len(slabs) - 1)
        for kh in range(2):
            multiply(first_values + 2, kh)
            multiply(first_values + 3, kh)
        add_terms(nc.vector, last_keys, 0, tile_result(last_keys))
        add_bias(first_values + 1)
        add_terms(nc.vector, last_keys, 2, tile_result(last_keys + 1))
        add_bias(first_values + 2)
        add_bias(first_values + 3)
